import numpy as np
import ml_dtypes


def mxq(x, axis, fmt="e4m3"):
    dtype, down = {"e4m3": (ml_dtypes.float8_e4m3fn, 7), "e5m2": (ml_dtypes.float8_e5m2, 14)}[fmt]
    v = np.moveaxis(np.asarray(x, np.float32).astype(ml_dtypes.bfloat16).astype(np.float64), axis, -1)
    blocks = v.reshape(v.shape[:-1] + (-1, 32))
    amax = np.abs(blocks).max(-1, keepdims=True)
    byte = np.maximum(np.where(amax > 0, np.frexp(amax)[1] - 1 + 127, 0) - down, 1)
    scale = np.exp2(byte - 127.0)
    codes = (blocks / scale).astype(np.float32).astype(dtype).astype(np.float64)
    return np.moveaxis((codes * scale).reshape(v.shape), -1, axis)


WIDE = False


def mx_kscale(k):
    if not WIDE:
        return np.ones(k)
    levels = np.array([10, -10, 5, -5, 0])
    if k % 512:
        return np.exp2(np.random.permutation(np.resize(levels, k // 32))).repeat(32)
    a = np.empty((k // 512, 16))
    for p in range(k // 512):
        a[p, :8] = np.random.permutation(np.resize(levels, 8))
        for g in range(8):
            far = levels[np.abs(levels - a[p, g]) >= 10]
            a[p, g + 8] = far[np.random.randint(len(far))]
    return np.exp2(a.ravel()).repeat(32)


BF16 = ml_dtypes.bfloat16


def bf(x):
    return np.asarray(x, np.float32).astype(BF16)


def f64(x):
    return np.asarray(x).astype(np.float64)


B, L, N, HID, H, D = 1, 128, 384, 1536, 12, 128


def apply_rope(x, rope):
    xp = x.reshape(x.shape[:-1] + (D // 2, 2))
    rp = rope[:, None].reshape(rope.shape[0], 1, rope.shape[1], D // 2, 2)
    cos, sin = rp[..., 0], rp[..., 1]
    x0, x1 = xp[..., 0], xp[..., 1]
    out = np.stack([x0 * cos - x1 * sin, x1 * cos + x0 * sin], axis=-1)
    return out.reshape(x.shape)


def setup_inputs():
    s = mx_kscale(HID)
    return {"img": bf(np.random.standard_normal((B, N, HID)) * s),
            "rope": bf(np.random.standard_normal((B, N, D))),
            "W_img_qkv": bf(np.random.standard_normal((3 * H * D, HID)) / np.sqrt(HID) / s)}


def reference(img, rope, W_img_qkv):
    y = mxq(f64(img), 2, "e4m3") @ mxq(f64(W_img_qkv), 1, "e4m3").T
    y = y.reshape(B, N, 3, H, D).transpose(2, 0, 3, 1, 4)
    r = f64(rope)
    return apply_rope(y[0], r), apply_rope(y[1], r), y[2]

@@ -1,0 +1,176 @@
+from contextlib import ExitStack
+
+from concourse import mybir
+from concourse.masks import make_identity
+
+F32 = mybir.dt.float32
+BF16 = mybir.dt.bfloat16
+U32 = mybir.dt.uint32
+U8 = mybir.dt.uint8
+FP8X4 = mybir.dt.float8_e4m3fn_x4
+MULT = mybir.AluOpType.mult
+ADD = mybir.AluOpType.add
+
+P = 128
+TOKENS = 384
+HID = 1536
+HEADS = 12
+D = 128
+K_PASS = 512
+PASSES = HID // K_PASS
+WORDS = HID // 2
+TOKEN_TILES = TOKENS // P
+GROUP_HEADS = 4
+GROUP_COLS = GROUP_HEADS * D
+HEAD_GROUPS = HEADS // GROUP_HEADS
+PAIRS = D // 2
+
+FLOPS = 2 * TOKENS * 3 * HEADS * D * HID
+
+
+def tile_jointattention_pa_kernel(tc, img, rope, w_qkv, out_q, out_k, out_v):
+    nc = tc.nc
+    outs = [o.rearrange("b h n d -> (b h) n d") for o in (out_q, out_k, out_v)]
+    groups = [(which, hg) for hg in range(HEAD_GROUPS) for which in range(3)]
+
+    with ExitStack() as stack:
+        const = stack.enter_context(tc.tile_pool(name="const", bufs=1))
+        w_pool = stack.enter_context(tc.tile_pool(name="w_rows", bufs=len(groups)))
+        grouped_pool = stack.enter_context(tc.tile_pool(name="grouped", bufs=4))
+        quant_pool = stack.enter_context(tc.tile_pool(name="quant", bufs=3))
+        rot_pool = stack.enter_context(tc.tile_pool(name="rot", bufs=3))
+        out_pool = stack.enter_context(tc.tile_pool(name="out", bufs=6))
+        flip_psum = stack.enter_context(tc.psum_pool(name="flip", bufs=4))
+        acc_psum = stack.enter_context(tc.psum_pool(name="acc", bufs=4))
+
+        img_sb = const.tile([P, TOKEN_TILES, HID], BF16)
+        nc.sync.dma_start(
+            out=img_sb[:], in_=img.flatten_outer_dims().rearrange("(p a) k -> p a k", a=TOKEN_TILES)
+        )
+        rope_sb = const.tile([P, TOKEN_TILES, D], BF16)
+        nc.scalar.dma_start(
+            out=rope_sb[:], in_=rope.flatten_outer_dims().rearrange("(p a) d -> p a d", a=TOKEN_TILES)
+        )
+        w_rows = []
+        for which, hg in groups:
+            first = which * HEADS * D + hg * GROUP_COLS
+            w_sb = w_pool.tile([P, GROUP_HEADS, HID], BF16, name="w_sb")
+            nc.sync.dma_start(
+                out=w_sb[:], in_=w_qkv[first : first + GROUP_COLS, :].rearrange("(h p) k -> p h k", p=P)
+            )
+            w_rows.append(w_sb)
+
+        ident = const.tile([P, P], F32)
+        make_identity(nc, ident[:])
+
+        rope_pairs = rope_sb[:].rearrange("p a (i e) -> p a i e", e=2)
+        cos_twice = const.tile([P, TOKEN_TILES, D], F32)
+        nc.vector.tensor_copy(
+            out=cos_twice[:].rearrange("p a (i e) -> p a i e", e=2),
+            in_=rope_pairs[:, :, :, 0:1].to_broadcast([P, TOKEN_TILES, PAIRS, 2]),
+        )
+        sin_signed = const.tile([P, 2, TOKEN_TILES, PAIRS], F32)
+        nc.vector.tensor_scalar_mul(out=sin_signed[:, 0], in0=rope_pairs[:, :, :, 1], scalar1=-1.0)
+        nc.vector.tensor_copy(out=sin_signed[:, 1], in_=rope_pairs[:, :, :, 1])
+
+        def k_onto_partitions(row_blocks, g, grouped_words):
+            width = P * len(row_blocks)
+            flipped = flip_psum.tile([P, 2, width], F32, name="flipped")
+            for u in range(2):
+                first_word = (K_PASS // 2) * g
+                for b, rows in enumerate(row_blocks):
+                    nc.tensor.transpose(
+                        flipped[:, u, b * P : (b + 1) * P],
+                        rows.bitcast(F32)[:, first_word + u : first_word + 2 * P : 2],
+                        ident[:],
+                    )
+            nc.scalar.copy(out=grouped_words, in_=flipped[:].rearrange("p u c -> p c u"))
+
+        def as_words(grouped):
+            return grouped[:].rearrange("p c v -> p (c v)").bitcast(F32).rearrange("p (c u) -> p c u", u=2)
+
+        img_codes = const.tile([P, PASSES, TOKENS], U32, align_bytes=64)
+        img_scales = const.tile([P, PASSES, TOKENS], U8, align_bytes=64)
+        for g in range(PASSES):
+            for a in range(TOKEN_TILES):
+                img_grouped = grouped_pool.tile([P, P, 4], BF16, align_bytes=64, name="img_grouped")
+                k_onto_partitions([img_sb[:, a, :]], g, as_words(img_grouped))
+                nc.vector.quantize_mx(
+                    out=img_codes[:, g, a * P : (a + 1) * P].bitcast(FP8X4),
+                    scales=img_scales[:, g, a * P : (a + 1) * P],
+                    in_=img_grouped[:].rearrange("p c v -> p (c v)"),
+                )
+
+        def quantise_group(n):
+            w_codes = quant_pool.tile([P, PASSES, GROUP_COLS], U32, align_bytes=64, name="w_codes")
+            w_scales = quant_pool.tile([P, PASSES, GROUP_COLS], U8, align_bytes=64, name="w_scales")
+            for g in range(PASSES):
+                w_grouped = grouped_pool.tile([P, GROUP_COLS, 4], BF16, align_bytes=64, name="w_grouped")
+                for h in range(0, GROUP_HEADS, 2):
+                    k_onto_partitions(
+                        [w_rows[n][:, h, :], w_rows[n][:, h + 1, :]],
+                        g,
+                        as_words(w_grouped)[:, h * P : (h + 2) * P, :],
+                    )
+                nc.vector.quantize_mx(
+                    out=w_codes[:, g, :].bitcast(FP8X4),
+                    scales=w_scales[:, g, :],
+                    in_=w_grouped[:].rearrange("p c v -> p (c v)"),
+                )
+            return w_codes, w_scales
+
+        def multiply_group(n, w_codes, w_scales):
+            which, hg = groups[n]
+            out_sb = out_pool.tile([P, GROUP_HEADS, TOKEN_TILES, D], F32, name="out_sb")
+            for a in range(TOKEN_TILES):
+                acc = acc_psum.tile([P, GROUP_COLS], F32, name="acc")
+                for g in range(PASSES):
+                    nc.tensor.matmul_mx(
+                        out=acc[:],
+                        lhsT=img_codes[:, g, a * P : (a + 1) * P].bitcast(FP8X4),
+                        lhsT_scale=img_scales[:, g, a * P : (a + 1) * P],
+                        rhs=w_codes[:, g, :].bitcast(FP8X4),
+                        rhs_scale=w_scales[:, g, :],
+                        start=(g == 0),
+                        stop=(g == PASSES - 1),
+                    )
+                result = out_sb[:, :, a, :]
+                by_head = acc[:].rearrange("p (h d) -> p h d", h=GROUP_HEADS)
+                if which == 2:
+                    nc.scalar.copy(out=result, in_=by_head)
+                    continue
+                by_pair = acc[:].rearrange("p (h i e) -> p h i e", h=GROUP_HEADS, e=2)
+                cross = rot_pool.tile([P, 2, GROUP_HEADS, PAIRS], F32, name="cross")
+                for e in range(2):
+                    nc.vector.tensor_tensor(
+                        out=cross[:, e],
+                        in0=by_pair[:, :, :, 1 - e],
+                        in1=sin_signed[:, e, a, :].unsqueeze(1).to_broadcast([P, GROUP_HEADS, PAIRS]),
+                        op=MULT,
+                    )
+                nc.vector.tensor_tensor(
+                    out=result,
+                    in0=by_head,
+                    in1=cos_twice[:, a, :].unsqueeze(1).to_broadcast([P, GROUP_HEADS, D]),
+                    op=MULT,
+                )
+                result_pairs = result.rearrange("p h (i e) -> p h i e", e=2)
+                nc.vector.tensor_tensor(
+                    out=result_pairs,
+                    in0=result_pairs,
+                    in1=cross[:].rearrange("p e h i -> p h i e"),
+                    op=ADD,
+                )
+            nc.sync.dma_start(
+                out=outs[which][hg * GROUP_HEADS : (hg + 1) * GROUP_HEADS].rearrange(
+                    "h (p a) d -> p h (a d)", a=TOKEN_TILES
+                ),
+                in_=out_sb[:].rearrange("p h a d -> p h (a d)"),
+            )
+
+        ready = quantise_group(0)
+        for n in range(1, len(groups)):
+            following = quantise_group(n)
+            multiply_group(n - 1, ready[0], ready[1])
+            ready = following
+        multiply_group(len(groups) - 1, ready[0], ready[1])

@@ -18,12 +18,14 @@ HEADS = 12
 D = 128
 K_PASS = 512
 PASSES = HID // K_PASS
-WORDS = HID // 2
 TOKEN_TILES = TOKENS // P
 GROUP_HEADS = 4
 GROUP_COLS = GROUP_HEADS * D
+HALF_HEADS = GROUP_HEADS // 2
+HALF_COLS = HALF_HEADS * D
 HEAD_GROUPS = HEADS // GROUP_HEADS
 PAIRS = D // 2
+V_PART = 2
 
 FLOPS = 2 * TOKENS * 3 * HEADS * D * HID
 
@@ -32,145 +34,214 @@ def tile_jointattention_pa_kernel(tc, img, rope, w_qkv, out_q, out_k, out_v):
     nc = tc.nc
     outs = [o.rearrange("b h n d -> (b h) n d") for o in (out_q, out_k, out_v)]
     groups = [(which, hg) for hg in range(HEAD_GROUPS) for which in range(3)]
+    last = len(groups) - 1
 
     with ExitStack() as stack:
         const = stack.enter_context(tc.tile_pool(name="const", bufs=1))
         w_pool = stack.enter_context(tc.tile_pool(name="w_rows", bufs=len(groups)))
         grouped_pool = stack.enter_context(tc.tile_pool(name="grouped", bufs=4))
         quant_pool = stack.enter_context(tc.tile_pool(name="quant", bufs=3))
-        rot_pool = stack.enter_context(tc.tile_pool(name="rot", bufs=3))
+        rot_pool = stack.enter_context(tc.tile_pool(name="rot", bufs=4))
         out_pool = stack.enter_context(tc.tile_pool(name="out", bufs=6))
         flip_psum = stack.enter_context(tc.psum_pool(name="flip", bufs=4))
         acc_psum = stack.enter_context(tc.psum_pool(name="acc", bufs=4))
-
-        img_sb = const.tile([P, TOKEN_TILES, HID], BF16)
-        nc.sync.dma_start(
-            out=img_sb[:], in_=img.flatten_outer_dims().rearrange("(p a) k -> p a k", a=TOKEN_TILES)
-        )
-        rope_sb = const.tile([P, TOKEN_TILES, D], BF16)
-        nc.scalar.dma_start(
-            out=rope_sb[:], in_=rope.flatten_outer_dims().rearrange("(p a) d -> p a d", a=TOKEN_TILES)
-        )
-        w_rows = []
-        for which, hg in groups:
-            first = which * HEADS * D + hg * GROUP_COLS
-            w_sb = w_pool.tile([P, GROUP_HEADS, HID], BF16, name="w_sb")
-            nc.sync.dma_start(
-                out=w_sb[:], in_=w_qkv[first : first + GROUP_COLS, :].rearrange("(h p) k -> p h k", p=P)
-            )
-            w_rows.append(w_sb)
+        stack.enter_context(tc.manual_schedule())
 
         ident = const.tile([P, P], F32)
         make_identity(nc, ident[:])
 
-        rope_pairs = rope_sb[:].rearrange("p a (i e) -> p a i e", e=2)
-        cos_twice = const.tile([P, TOKEN_TILES, D], F32)
-        nc.vector.tensor_copy(
-            out=cos_twice[:].rearrange("p a (i e) -> p a i e", e=2),
-            in_=rope_pairs[:, :, :, 0:1].to_broadcast([P, TOKEN_TILES, PAIRS, 2]),
-        )
-        sin_signed = const.tile([P, 2, TOKEN_TILES, PAIRS], F32)
-        nc.vector.tensor_scalar_mul(out=sin_signed[:, 0], in0=rope_pairs[:, :, :, 1], scalar1=-1.0)
-        nc.vector.tensor_copy(out=sin_signed[:, 1], in_=rope_pairs[:, :, :, 1])
+        img_rows = img.flatten_outer_dims().rearrange("(p a) k -> p a k", a=TOKEN_TILES)
+        img_sb = []
+        for a in range(TOKEN_TILES):
+            rows_sb = const.tile([P, HID], BF16, name=f"img_sb{a}")
+            nc.sync.dma_start(out=rows_sb[:], in_=img_rows[:, a, :])
+            img_sb.append(rows_sb)
+        rope_sb = const.tile([P, TOKEN_TILES, D], BF16)
+        w_halves = []
+        for n, (which, hg) in enumerate(groups):
+            first = which * HEADS * D + hg * GROUP_COLS
+            halves = []
+            for half in range(2):
+                w_sb = w_pool.tile([P, HALF_HEADS, HID], BF16, name=f"w_sb{half}")
+                first_row = first + half * HALF_COLS
+                nc.sync.dma_start(
+                    out=w_sb[:],
+                    in_=w_qkv[first_row : first_row + HALF_COLS, :].rearrange("(h p) k -> p h k", p=P),
+                )
+                halves.append(w_sb)
+            w_halves.append(halves)
+            if n == 0:
+                nc.sync.dma_start(
+                    out=rope_sb[:], in_=rope.flatten_outer_dims().rearrange("(p a) d -> p a d", a=TOKEN_TILES)
+                )
 
-        def k_onto_partitions(row_blocks, g, grouped_words):
-            width = P * len(row_blocks)
-            flipped = flip_psum.tile([P, 2, width], F32, name="flipped")
+        def transpose_pass(flipped, rows, g):
+            first_word = (K_PASS // 2) * g
             for u in range(2):
-                first_word = (K_PASS // 2) * g
-                for b, rows in enumerate(row_blocks):
-                    nc.tensor.transpose(
-                        flipped[:, u, b * P : (b + 1) * P],
-                        rows.bitcast(F32)[:, first_word + u : first_word + 2 * P : 2],
-                        ident[:],
-                    )
-            nc.scalar.copy(out=grouped_words, in_=flipped[:].rearrange("p u c -> p c u"))
+                nc.tensor.transpose(
+                    flipped[:, u, :], rows.bitcast(F32)[:, first_word + u : first_word + 2 * P : 2], ident[:]
+                )
 
         def as_words(grouped):
-            return grouped[:].rearrange("p c v -> p (c v)").bitcast(F32).rearrange("p (c u) -> p c u", u=2)
+            return grouped.rearrange("p c v -> p (c v)").bitcast(F32).rearrange("p (c u) -> p c u", u=2)
 
-        img_codes = const.tile([P, PASSES, TOKENS], U32, align_bytes=64)
-        img_scales = const.tile([P, PASSES, TOKENS], U8, align_bytes=64)
-        for g in range(PASSES):
-            for a in range(TOKEN_TILES):
-                img_grouped = grouped_pool.tile([P, P, 4], BF16, align_bytes=64, name="img_grouped")
-                k_onto_partitions([img_sb[:, a, :]], g, as_words(img_grouped))
+        img_codes = const.tile([P, TOKEN_TILES, PASSES, P], U32, align_bytes=64)
+        img_scales = const.tile([P, TOKEN_TILES, PASSES, P], U8, align_bytes=64)
+        for a in range(TOKEN_TILES):
+            for first_g, count in ((0, 2), (2, 1)):
+                flipped = flip_psum.tile([P, 2, 2, P], F32, name="flipped")
+                for j in range(count):
+                    transpose_pass(flipped[:, j], img_sb[a][:], first_g + j)
+                img_grouped = grouped_pool.tile([P, count, P, 4], BF16, align_bytes=64, name=f"img_grouped{count}")
+                nc.scalar.copy(
+                    out=as_words(img_grouped[:].rearrange("p j c v -> p (j c) v")).rearrange(
+                        "p (j c) u -> p j c u", j=count
+                    ),
+                    in_=flipped[:, 0:count].rearrange("p j u c -> p j c u"),
+                )
                 nc.vector.quantize_mx(
-                    out=img_codes[:, g, a * P : (a + 1) * P].bitcast(FP8X4),
-                    scales=img_scales[:, g, a * P : (a + 1) * P],
-                    in_=img_grouped[:].rearrange("p c v -> p (c v)"),
+                    out=img_codes[:, a, first_g : first_g + count, :].rearrange("p g c -> p (g c)").bitcast(FP8X4),
+                    scales=img_scales[:, a, first_g : first_g + count, :].rearrange("p g c -> p (g c)"),
+                    in_=img_grouped[:].rearrange("p j c v -> p (j c v)"),
                 )
 
-        def quantise_group(n):
-            w_codes = quant_pool.tile([P, PASSES, GROUP_COLS], U32, align_bytes=64, name="w_codes")
-            w_scales = quant_pool.tile([P, PASSES, GROUP_COLS], U8, align_bytes=64, name="w_scales")
-            for g in range(PASSES):
-                w_grouped = grouped_pool.tile([P, GROUP_COLS, 4], BF16, align_bytes=64, name="w_grouped")
-                for h in range(0, GROUP_HEADS, 2):
-                    k_onto_partitions(
-                        [w_rows[n][:, h, :], w_rows[n][:, h + 1, :]],
-                        g,
-                        as_words(w_grouped)[:, h * P : (h + 2) * P, :],
-                    )
-                nc.vector.quantize_mx(
-                    out=w_codes[:, g, :].bitcast(FP8X4),
-                    scales=w_scales[:, g, :],
-                    in_=w_grouped[:].rearrange("p c v -> p (c v)"),
-                )
-            return w_codes, w_scales
+        rope_pairs = rope_sb[:].rearrange("p a (i e) -> p a i e", e=2)
+        cos_twice = const.tile([P, TOKEN_TILES, D], F32)
+        sin_signed = const.tile([P, TOKEN_TILES, PAIRS, 2], F32)
 
-        def multiply_group(n, w_codes, w_scales):
-            which, hg = groups[n]
-            out_sb = out_pool.tile([P, GROUP_HEADS, TOKEN_TILES, D], F32, name="out_sb")
-            for a in range(TOKEN_TILES):
-                acc = acc_psum.tile([P, GROUP_COLS], F32, name="acc")
-                for g in range(PASSES):
-                    nc.tensor.matmul_mx(
-                        out=acc[:],
-                        lhsT=img_codes[:, g, a * P : (a + 1) * P].bitcast(FP8X4),
-                        lhsT_scale=img_scales[:, g, a * P : (a + 1) * P],
-                        rhs=w_codes[:, g, :].bitcast(FP8X4),
-                        rhs_scale=w_scales[:, g, :],
-                        start=(g == 0),
-                        stop=(g == PASSES - 1),
-                    )
-                result = out_sb[:, :, a, :]
-                by_head = acc[:].rearrange("p (h d) -> p h d", h=GROUP_HEADS)
-                if which == 2:
-                    nc.scalar.copy(out=result, in_=by_head)
-                    continue
-                by_pair = acc[:].rearrange("p (h i e) -> p h i e", h=GROUP_HEADS, e=2)
-                cross = rot_pool.tile([P, 2, GROUP_HEADS, PAIRS], F32, name="cross")
-                for e in range(2):
-                    nc.vector.tensor_tensor(
-                        out=cross[:, e],
-                        in0=by_pair[:, :, :, 1 - e],
-                        in1=sin_signed[:, e, a, :].unsqueeze(1).to_broadcast([P, GROUP_HEADS, PAIRS]),
-                        op=MULT,
-                    )
-                nc.vector.tensor_tensor(
-                    out=result,
-                    in0=by_head,
-                    in1=cos_twice[:, a, :].unsqueeze(1).to_broadcast([P, GROUP_HEADS, D]),
-                    op=MULT,
+        def make_tables():
+            nc.vector.tensor_copy(
+                out=cos_twice[:].rearrange("p a (i e) -> p a i e", e=2),
+                in_=rope_pairs[:, :, :, 0:1].to_broadcast([P, TOKEN_TILES, PAIRS, 2]),
+            )
+            nc.vector.tensor_scalar_mul(out=sin_signed[:, :, :, 0], in0=rope_pairs[:, :, :, 1], scalar1=-1.0)
+            nc.vector.tensor_copy(out=sin_signed[:, :, :, 1], in_=rope_pairs[:, :, :, 1])
+
+        grouped_tiles = {}
+        codes = {}
+        results = {}
+        crosses = {}
+
+        def flip(n, g, half):
+            if (n, g) not in grouped_tiles:
+                grouped_tiles[n, g] = grouped_pool.tile(
+                    [P, GROUP_COLS, 4], BF16, align_bytes=64, name="w_grouped"
                 )
-                result_pairs = result.rearrange("p h (i e) -> p h i e", e=2)
-                nc.vector.tensor_tensor(
-                    out=result_pairs,
-                    in0=result_pairs,
-                    in1=cross[:].rearrange("p e h i -> p h i e"),
-                    op=ADD,
-                )
-            nc.sync.dma_start(
-                out=outs[which][hg * GROUP_HEADS : (hg + 1) * GROUP_HEADS].rearrange(
-                    "h (p a) d -> p h (a d)", a=TOKEN_TILES
-                ),
-                in_=out_sb[:].rearrange("p h a d -> p h (a d)"),
+            flipped = flip_psum.tile([P, 2, 2, P], F32, name="flipped")
+            for h in range(HALF_HEADS):
+                transpose_pass(flipped[:, h], w_halves[n][half][:, h, :], g)
+            words = as_words(grouped_tiles[n, g][:])[:, half * HALF_COLS : (half + 1) * HALF_COLS, :]
+            nc.scalar.copy(
+                out=words.rearrange("p (h c) u -> p h c u", h=HALF_HEADS),
+                in_=flipped[:].rearrange("p h u c -> p h c u"),
             )
 
-        ready = quantise_group(0)
-        for n in range(1, len(groups)):
-            following = quantise_group(n)
-            multiply_group(n - 1, ready[0], ready[1])
-            ready = following
-        multiply_group(len(groups) - 1, ready[0], ready[1])
+        def quantise(n, g):
+            if n not in codes:
+                codes[n] = (
+                    quant_pool.tile([P, PASSES, GROUP_COLS], U32, align_bytes=64, name="w_codes"),
+                    quant_pool.tile([P, PASSES, GROUP_COLS], U8, align_bytes=64, name="w_scales"),
+                )
+            nc.vector.quantize_mx(
+                out=codes[n][0][:, g, :].bitcast(FP8X4),
+                scales=codes[n][1][:, g, :],
+                in_=grouped_tiles.pop((n, g))[:].rearrange("p c v -> p (c v)"),
+            )
+
+        def multiply(n, a, first_col, width):
+            acc = acc_psum.tile([P, GROUP_COLS], F32, name="acc")
+            cols = slice(first_col, first_col + width)
+            for g in range(PASSES):
+                nc.tensor.matmul_mx(
+                    out=acc[:, 0:width],
+                    lhsT=img_codes[:, a, g, :].bitcast(FP8X4),
+                    lhsT_scale=img_scales[:, a, g, :],
+                    rhs=codes[n][0][:, g, cols].bitcast(FP8X4),
+                    rhs_scale=codes[n][1][:, g, cols],
+                    start=(g == 0),
+                    stop=(g == PASSES - 1),
+                )
+            return acc
+
+        def result_tile(n):
+            if n not in results:
+                results[n] = out_pool.tile([P, GROUP_HEADS, TOKEN_TILES, D], F32, name="out_sb")
+            return results[n]
+
+        def empty_bank(n, a, acc):
+            result = result_tile(n)[:, :, a, :]
+            by_head = acc[:].rearrange("p (h d) -> p h d", h=GROUP_HEADS)
+            if groups[n][0] == V_PART:
+                nc.scalar.copy(out=result, in_=by_head)
+                return
+            cross = rot_pool.tile([P, GROUP_HEADS, PAIRS, 2], F32, name="cross")
+            crosses[n, a] = cross
+            nc.vector.tensor_tensor(
+                out=cross[:],
+                in0=acc[:].rearrange("p (h i e) -> p h i e", h=GROUP_HEADS, e=2)[:, :, :, ::-1],
+                in1=sin_signed[:, a].unsqueeze(1).to_broadcast([P, GROUP_HEADS, PAIRS, 2]),
+                op=MULT,
+            )
+            nc.vector.tensor_tensor(
+                out=result,
+                in0=by_head,
+                in1=cos_twice[:, a, :].unsqueeze(1).to_broadcast([P, GROUP_HEADS, D]),
+                op=MULT,
+            )
+
+        def add_products(n, a):
+            if groups[n][0] == V_PART:
+                return
+            result = result_tile(n)[:, :, a, :]
+            cross = crosses.pop((n, a))
+            nc.vector.tensor_tensor(
+                out=result, in0=result, in1=cross[:].rearrange("p h i e -> p h (i e)"), op=ADD
+            )
+
+        def store(n, first_head, heads):
+            which, hg = groups[n]
+            head = hg * GROUP_HEADS + first_head
+            nc.sync.dma_start(
+                out=outs[which][head : head + heads].rearrange("h (p a) d -> p h (a d)", a=TOKEN_TILES),
+                in_=result_tile(n)[:, first_head : first_head + heads].rearrange("p h a d -> p h (a d)"),
+            )
+
+        for half in range(2):
+            for g in range(PASSES):
+                flip(0, g, half)
+        make_tables()
+        for g in range(PASSES):
+            quantise(0, g)
+        for n in range(last):
+            m = n + 1
+            for g in range(2):
+                for half in range(2):
+                    flip(m, g, half)
+            if n > 0:
+                add_products(n - 1, 2)
+                store(n - 1, 0, GROUP_HEADS)
+            quantise(m, 0)
+            acc0 = multiply(n, 0, 0, GROUP_COLS)
+            acc1 = multiply(n, 1, 0, GROUP_COLS)
+            quantise(m, 1)
+            for half in range(2):
+                flip(m, 2, half)
+            acc2 = multiply(n, 2, 0, GROUP_COLS)
+            empty_bank(n, 0, acc0)
+            empty_bank(n, 1, acc1)
+            quantise(m, 2)
+            add_products(n, 0)
+            empty_bank(n, 2, acc2)
+            add_products(n, 1)
+        add_products(last - 1, 2)
+        store(last - 1, 0, GROUP_HEADS)
+        for half in range(2):
+            for a in range(TOKEN_TILES):
+                acc = multiply(last, a, half * HALF_COLS, HALF_COLS)
+                heads = slice(half * HALF_HEADS, (half + 1) * HALF_HEADS)
+                copy = nc.vector.tensor_copy if (half + a) % 2 else nc.scalar.copy
+                copy(
+                    out=result_tile(last)[:, heads, a, :],
+                    in_=acc[:, 0:HALF_COLS].rearrange("p (h d) -> p h d", h=HALF_HEADS),
+                )
+            store(last, half * HALF_HEADS, HALF_HEADS)

@@ -26,6 +26,7 @@ HALF_COLS = HALF_HEADS * D
 HEAD_GROUPS = HEADS // GROUP_HEADS
 PAIRS = D // 2
 V_PART = 2
+LAG = 1
 
 FLOPS = 2 * TOKENS * 3 * HEADS * D * HID
 
@@ -206,34 +207,28 @@ def tile_jointattention_pa_kernel(tc, img, rope, w_qkv, out_q, out_k, out_v):
                 in_=result_tile(n)[:, first_head : first_head + heads].rearrange("p h a d -> p h (a d)"),
             )
 
-        for half in range(2):
-            for g in range(PASSES):
-                flip(0, g, half)
-        make_tables()
-        for g in range(PASSES):
-            quantise(0, g)
-        for n in range(last):
-            m = n + 1
-            for g in range(2):
+        flips = [(n, g) for n in range(last + 1) for g in range(PASSES)]
+        products = [(n, a) for n in range(last) for a in range(TOKEN_TILES)]
+        unsummed = []
+        for turn in range(len(products) + PASSES + LAG):
+            if turn < len(flips):
+                n, g = flips[turn]
                 for half in range(2):
-                    flip(m, g, half)
-            if n > 0:
-                add_products(n - 1, 2)
-                store(n - 1, 0, GROUP_HEADS)
-            quantise(m, 0)
-            acc0 = multiply(n, 0, 0, GROUP_COLS)
-            acc1 = multiply(n, 1, 0, GROUP_COLS)
-            quantise(m, 1)
-            for half in range(2):
-                flip(m, 2, half)
-            acc2 = multiply(n, 2, 0, GROUP_COLS)
-            empty_bank(n, 0, acc0)
-            empty_bank(n, 1, acc1)
-            quantise(m, 2)
-            add_products(n, 0)
-            empty_bank(n, 2, acc2)
-            add_products(n, 1)
-        add_products(last - 1, 2)
+                    flip(n, g, half)
+                if turn == 0:
+                    make_tables()
+                quantise(n, g)
+            if turn >= PASSES + LAG:
+                n, a = products[turn - PASSES - LAG]
+                acc = multiply(n, a, 0, GROUP_COLS)
+                for done in unsummed:
+                    add_products(*done)
+                    if done[1] == TOKEN_TILES - 1:
+                        store(done[0], 0, GROUP_HEADS)
+                unsummed = [(n, a)]
+                empty_bank(n, a, acc)
+        for done in unsummed:
+            add_products(*done)
         store(last - 1, 0, GROUP_HEADS)
         for half in range(2):
             for a in range(TOKEN_TILES):

@@ -23,7 +23,6 @@ GROUP_HEADS = 4
 GROUP_COLS = GROUP_HEADS * D
 HALF_HEADS = GROUP_HEADS // 2
 HALF_COLS = HALF_HEADS * D
-HEAD_GROUPS = HEADS // GROUP_HEADS
 PAIRS = D // 2
 V_PART = 2
 LAG = 1
@@ -34,7 +33,7 @@ FLOPS = 2 * TOKENS * 3 * HEADS * D * HID
 def tile_jointattention_pa_kernel(tc, img, rope, w_qkv, out_q, out_k, out_v):
     nc = tc.nc
     outs = [o.rearrange("b h n d -> (b h) n d") for o in (out_q, out_k, out_v)]
-    groups = [(which, hg) for hg in range(HEAD_GROUPS) for which in range(3)]
+    groups = [(0, 0), (1, 0), (0, 1), (1, 1), (2, 0), (0, 2), (1, 2), (2, 1), (2, 2)]
     last = len(groups) - 1
 
     with ExitStack() as stack:

@@ -25,6 +25,7 @@ HALF_HEADS = GROUP_HEADS // 2
 HALF_COLS = HALF_HEADS * D
 PAIRS = D // 2
 V_PART = 2
+GPSIMD_SUMS = 2
 LAG = 1
 
 FLOPS = 2 * TOKENS * 3 * HEADS * D * HID
@@ -194,7 +195,8 @@ def tile_jointattention_pa_kernel(tc, img, rope, w_qkv, out_q, out_k, out_v):
                 return
             result = result_tile(n)[:, :, a, :]
             cross = crosses.pop((n, a))
-            nc.vector.tensor_tensor(
+            engine = nc.gpsimd if a < GPSIMD_SUMS else nc.vector
+            engine.tensor_tensor(
                 out=result, in0=result, in1=cross[:].rearrange("p h i e -> p h (i e)"), op=ADD
             )
 

@@ -25,6 +25,7 @@ HALF_HEADS = GROUP_HEADS // 2
 HALF_COLS = HALF_HEADS * D
 PAIRS = D // 2
 V_PART = 2
+ROTATED = 3
 GPSIMD_SUMS = 2
 LAG = 1
 
@@ -34,7 +35,9 @@ FLOPS = 2 * TOKENS * 3 * HEADS * D * HID
 def tile_jointattention_pa_kernel(tc, img, rope, w_qkv, out_q, out_k, out_v):
     nc = tc.nc
     outs = [o.rearrange("b h n d -> (b h) n d") for o in (out_q, out_k, out_v)]
-    groups = [(0, 0), (1, 0), (0, 1), (1, 1), (2, 0), (0, 2), (1, 2), (2, 1), (2, 2)]
+    rotated = [(part, head) for part in range(V_PART) for head in range(HEADS)]
+    groups = [rotated[ROTATED * n : ROTATED * (n + 1)] + [(V_PART, n)] for n in range(len(rotated) // ROTATED)]
+    groups.append([(V_PART, head) for head in range(len(groups), HEADS)])
     last = len(groups) - 1
 
     with ExitStack() as stack:
@@ -59,16 +62,19 @@ def tile_jointattention_pa_kernel(tc, img, rope, w_qkv, out_q, out_k, out_v):
             img_sb.append(rows_sb)
         rope_sb = const.tile([P, TOKEN_TILES, D], BF16)
         w_halves = []
-        for n, (which, hg) in enumerate(groups):
-            first = which * HEADS * D + hg * GROUP_COLS
+        for n, heads in enumerate(groups):
             halves = []
             for half in range(2):
                 w_sb = w_pool.tile([P, HALF_HEADS, HID], BF16, name=f"w_sb{half}")
-                first_row = first + half * HALF_COLS
-                nc.sync.dma_start(
-                    out=w_sb[:],
-                    in_=w_qkv[first_row : first_row + HALF_COLS, :].rearrange("(h p) k -> p h k", p=P),
-                )
+                pair = heads[half * HALF_HEADS : (half + 1) * HALF_HEADS]
+                neighbours = pair[0][0] == pair[1][0]
+                for h, count in [(0, 2)] if neighbours else [(0, 1), (1, 1)]:
+                    part, head = pair[h]
+                    first_row = (part * HEADS + head) * D
+                    nc.sync.dma_start(
+                        out=w_sb[:, h : h + count, :],
+                        in_=w_qkv[first_row : first_row + count * D, :].rearrange("(h p) k -> p h k", p=P),
+                    )
                 halves.append(w_sb)
             w_halves.append(halves)
             if n == 0:
@@ -170,30 +176,26 @@ def tile_jointattention_pa_kernel(tc, img, rope, w_qkv, out_q, out_k, out_v):
             return results[n]
 
         def empty_bank(n, a, acc):
-            result = result_tile(n)[:, :, a, :]
             by_head = acc[:].rearrange("p (h d) -> p h d", h=GROUP_HEADS)
-            if groups[n][0] == V_PART:
-                nc.scalar.copy(out=result, in_=by_head)
-                return
-            cross = rot_pool.tile([P, GROUP_HEADS, PAIRS, 2], F32, name="cross")
+            nc.scalar.copy(out=result_tile(n)[:, ROTATED:, a, :], in_=by_head[:, ROTATED:, :])
+            result = result_tile(n)[:, 0:ROTATED, a, :]
+            cross = rot_pool.tile([P, ROTATED, PAIRS, 2], F32, name="cross")
             crosses[n, a] = cross
             nc.vector.tensor_tensor(
                 out=cross[:],
-                in0=acc[:].rearrange("p (h i e) -> p h i e", h=GROUP_HEADS, e=2)[:, :, :, ::-1],
-                in1=sin_signed[:, a].unsqueeze(1).to_broadcast([P, GROUP_HEADS, PAIRS, 2]),
+                in0=by_head[:, 0:ROTATED, :].rearrange("p h (i e) -> p h i e", e=2)[:, :, :, ::-1],
+                in1=sin_signed[:, a].unsqueeze(1).to_broadcast([P, ROTATED, PAIRS, 2]),
                 op=MULT,
             )
             nc.vector.tensor_tensor(
                 out=result,
-                in0=by_head,
-                in1=cos_twice[:, a, :].unsqueeze(1).to_broadcast([P, GROUP_HEADS, D]),
+                in0=by_head[:, 0:ROTATED, :],
+                in1=cos_twice[:, a, :].unsqueeze(1).to_broadcast([P, ROTATED, D]),
                 op=MULT,
             )
 
         def add_products(n, a):
-            if groups[n][0] == V_PART:
-                return
-            result = result_tile(n)[:, :, a, :]
+            result = result_tile(n)[:, 0:ROTATED, a, :]
             cross = crosses.pop((n, a))
             engine = nc.gpsimd if a < GPSIMD_SUMS else nc.vector
             engine.tensor_tensor(
@@ -201,12 +203,15 @@ def tile_jointattention_pa_kernel(tc, img, rope, w_qkv, out_q, out_k, out_v):
             )
 
         def store(n, first_head, heads):
-            which, hg = groups[n]
-            head = hg * GROUP_HEADS + first_head
+            which, head = groups[n][first_head]
             nc.sync.dma_start(
                 out=outs[which][head : head + heads].rearrange("h (p a) d -> p h (a d)", a=TOKEN_TILES),
                 in_=result_tile(n)[:, first_head : first_head + heads].rearrange("p h a d -> p h (a d)"),
             )
+
+        def store_group(n):
+            store(n, ROTATED, GROUP_HEADS - ROTATED)
+            store(n, 0, ROTATED)
 
         flips = [(n, g) for n in range(last + 1) for g in range(PASSES)]
         products = [(n, a) for n in range(last) for a in range(TOKEN_TILES)]
@@ -225,12 +230,12 @@ def tile_jointattention_pa_kernel(tc, img, rope, w_qkv, out_q, out_k, out_v):
                 for done in unsummed:
                     add_products(*done)
                     if done[1] == TOKEN_TILES - 1:
-                        store(done[0], 0, GROUP_HEADS)
+                        store_group(done[0])
                 unsummed = [(n, a)]
                 empty_bank(n, a, acc)
         for done in unsummed:
             add_products(*done)
-        store(last - 1, 0, GROUP_HEADS)
+        store_group(last - 1)
         for half in range(2):
             for a in range(TOKEN_TILES):
                 acc = multiply(last, a, half * HALF_COLS, HALF_COLS)

@@ -27,7 +27,6 @@ PAIRS = D // 2
 V_PART = 2
 ROTATED = 3
 GPSIMD_SUMS = 2
-LAG = 1
 
 FLOPS = 2 * TOKENS * 3 * HEADS * D * HID
 
@@ -43,7 +42,8 @@ def tile_jointattention_pa_kernel(tc, img, rope, w_qkv, out_q, out_k, out_v):
     with ExitStack() as stack:
         const = stack.enter_context(tc.tile_pool(name="const", bufs=1))
         w_pool = stack.enter_context(tc.tile_pool(name="w_rows", bufs=len(groups)))
-        grouped_pool = stack.enter_context(tc.tile_pool(name="grouped", bufs=4))
+        grouped_pool = stack.enter_context(tc.tile_pool(name="grouped", bufs=7))
+        img_grouped_pool = stack.enter_context(tc.tile_pool(name="img_grouped", bufs=2))
         quant_pool = stack.enter_context(tc.tile_pool(name="quant", bufs=3))
         rot_pool = stack.enter_context(tc.tile_pool(name="rot", bufs=4))
         out_pool = stack.enter_context(tc.tile_pool(name="out", bufs=6))
@@ -99,7 +99,7 @@ def tile_jointattention_pa_kernel(tc, img, rope, w_qkv, out_q, out_k, out_v):
                 flipped = flip_psum.tile([P, 2, 2, P], F32, name="flipped")
                 for j in range(count):
                     transpose_pass(flipped[:, j], img_sb[a][:], first_g + j)
-                img_grouped = grouped_pool.tile([P, count, P, 4], BF16, align_bytes=64, name=f"img_grouped{count}")
+                img_grouped = img_grouped_pool.tile([P, count, P, 4], BF16, align_bytes=64, name=f"img_grouped{count}")
                 nc.scalar.copy(
                     out=as_words(img_grouped[:].rearrange("p j c v -> p (j c) v")).rearrange(
                         "p (j c) u -> p j c u", j=count
@@ -156,7 +156,10 @@ def tile_jointattention_pa_kernel(tc, img, rope, w_qkv, out_q, out_k, out_v):
             )
 
         def multiply(n, a, first_col, width):
-            acc = acc_psum.tile([P, GROUP_COLS], F32, name="acc")
+            if n == last and (first_col == 0 or a == 0):
+                acc = flip_psum.tile([P, 2, 2, P], F32, name="flipped")[:].rearrange("p h u c -> p (h u c)")
+            else:
+                acc = acc_psum.tile([P, GROUP_COLS], F32, name="acc")[:]
             cols = slice(first_col, first_col + width)
             for g in range(PASSES):
                 nc.tensor.matmul_mx(
@@ -176,7 +179,7 @@ def tile_jointattention_pa_kernel(tc, img, rope, w_qkv, out_q, out_k, out_v):
             return results[n]
 
         def empty_bank(n, a, acc):
-            by_head = acc[:].rearrange("p (h d) -> p h d", h=GROUP_HEADS)
+            by_head = acc.rearrange("p (h d) -> p h d", h=GROUP_HEADS)
             nc.scalar.copy(out=result_tile(n)[:, ROTATED:, a, :], in_=by_head[:, ROTATED:, :])
             result = result_tile(n)[:, 0:ROTATED, a, :]
             cross = rot_pool.tile([P, ROTATED, PAIRS, 2], F32, name="cross")
@@ -204,7 +207,8 @@ def tile_jointattention_pa_kernel(tc, img, rope, w_qkv, out_q, out_k, out_v):
 
         def store(n, first_head, heads):
             which, head = groups[n][first_head]
-            nc.sync.dma_start(
+            engine = nc.scalar if n == last else nc.sync
+            engine.dma_start(
                 out=outs[which][head : head + heads].rearrange("h (p a) d -> p h (a d)", a=TOKEN_TILES),
                 in_=result_tile(n)[:, first_head : first_head + heads].rearrange("p h a d -> p h (a d)"),
             )
@@ -213,35 +217,50 @@ def tile_jointattention_pa_kernel(tc, img, rope, w_qkv, out_q, out_k, out_v):
             store(n, ROTATED, GROUP_HEADS - ROTATED)
             store(n, 0, ROTATED)
 
-        flips = [(n, g) for n in range(last + 1) for g in range(PASSES)]
         products = [(n, a) for n in range(last) for a in range(TOKEN_TILES)]
         unsummed = []
-        for turn in range(len(products) + PASSES + LAG):
-            if turn < len(flips):
-                n, g = flips[turn]
+
+        def sum_products():
+            for n, a in unsummed:
+                add_products(n, a)
+                if a == TOKEN_TILES - 1:
+                    store_group(n)
+            unsummed.clear()
+
+        def take_product():
+            n, a = products[0]
+            products.remove(products[0])
+            acc = multiply(n, a, 0, GROUP_COLS)
+            sum_products()
+            unsummed.append((n, a))
+            empty_bank(n, a, acc)
+
+        for n in range(2):
+            for half in range(2):
+                for g in range(PASSES):
+                    flip(n, g, half)
+                    if n == 0 and half == 0 and g == 0:
+                        make_tables()
+                    if half == 1:
+                        quantise(n, g)
+                if n == 1:
+                    for i in range(2 * half):
+                        take_product()
+        for n in range(2, last + 1):
+            for g in range(PASSES):
                 for half in range(2):
                     flip(n, g, half)
-                if turn == 0:
-                    make_tables()
                 quantise(n, g)
-            if turn >= PASSES + LAG:
-                n, a = products[turn - PASSES - LAG]
-                acc = multiply(n, a, 0, GROUP_COLS)
-                for done in unsummed:
-                    add_products(*done)
-                    if done[1] == TOKEN_TILES - 1:
-                        store_group(done[0])
-                unsummed = [(n, a)]
-                empty_bank(n, a, acc)
-        for done in unsummed:
-            add_products(*done)
-        store_group(last - 1)
+                if (n, g) != (2, 0):
+                    take_product()
+        while products:
+            take_product()
+        sum_products()
         for half in range(2):
             for a in range(TOKEN_TILES):
                 acc = multiply(last, a, half * HALF_COLS, HALF_COLS)
                 heads = slice(half * HALF_HEADS, (half + 1) * HALF_HEADS)
-                copy = nc.vector.tensor_copy if (half + a) % 2 else nc.scalar.copy
-                copy(
+                nc.scalar.copy(
                     out=result_tile(last)[:, heads, a, :],
                     in_=acc[:, 0:HALF_COLS].rearrange("p (h d) -> p h d", h=HALF_HEADS),
                 )

@@ -25,8 +25,9 @@ HALF_HEADS = GROUP_HEADS // 2
 HALF_COLS = HALF_HEADS * D
 PAIRS = D // 2
 V_PART = 2
-ROTATED = 3
+ROTATED = (4, 4, 4, 3, 3, 2, 2, 2, 0)
 GPSIMD_SUMS = 2
+SORT_AHEAD = 3
 
 FLOPS = 2 * TOKENS * 3 * HEADS * D * HID
 
@@ -35,8 +36,12 @@ def tile_jointattention_pa_kernel(tc, img, rope, w_qkv, out_q, out_k, out_v):
     nc = tc.nc
     outs = [o.rearrange("b h n d -> (b h) n d") for o in (out_q, out_k, out_v)]
     rotated = [(part, head) for part in range(V_PART) for head in range(HEADS)]
-    groups = [rotated[ROTATED * n : ROTATED * (n + 1)] + [(V_PART, n)] for n in range(len(rotated) // ROTATED)]
-    groups.append([(V_PART, head) for head in range(len(groups), HEADS)])
+    others = [(V_PART, head) for head in range(HEADS)]
+    groups = []
+    for n, count in enumerate(ROTATED):
+        first = sum(ROTATED[:n])
+        first_v = GROUP_HEADS * n - first
+        groups.append(rotated[first : first + count] + others[first_v : first_v + GROUP_HEADS - count])
     last = len(groups) - 1
 
     with ExitStack() as stack:
@@ -45,6 +50,7 @@ def tile_jointattention_pa_kernel(tc, img, rope, w_qkv, out_q, out_k, out_v):
         grouped_pool = stack.enter_context(tc.tile_pool(name="grouped", bufs=7))
         img_grouped_pool = stack.enter_context(tc.tile_pool(name="img_grouped", bufs=2))
         quant_pool = stack.enter_context(tc.tile_pool(name="quant", bufs=3))
+        sorted_pool = stack.enter_context(tc.tile_pool(name="sorted", bufs=4))
         rot_pool = stack.enter_context(tc.tile_pool(name="rot", bufs=4))
         out_pool = stack.enter_context(tc.tile_pool(name="out", bufs=6))
         flip_psum = stack.enter_context(tc.psum_pool(name="flip", bufs=4))
@@ -129,6 +135,19 @@ def tile_jointattention_pa_kernel(tc, img, rope, w_qkv, out_q, out_k, out_v):
         results = {}
         crosses = {}
 
+        sorted_words = {}
+
+        def sort_words(n, g):
+            tile = sorted_pool.tile([P, HALF_HEADS, 2, P], F32, name="sorted")
+            sorted_words[n, g] = tile
+            first_word = (K_PASS // 2) * g
+            nc.scalar.copy(
+                out=tile[:],
+                in_=w_halves[n][0][:].bitcast(F32)[:, :, first_word : first_word + 2 * P].rearrange(
+                    "p h (q u) -> p h u q", u=2
+                ),
+            )
+
         def flip(n, g, half):
             if (n, g) not in grouped_tiles:
                 grouped_tiles[n, g] = grouped_pool.tile(
@@ -136,7 +155,11 @@ def tile_jointattention_pa_kernel(tc, img, rope, w_qkv, out_q, out_k, out_v):
                 )
             flipped = flip_psum.tile([P, 2, 2, P], F32, name="flipped")
             for h in range(HALF_HEADS):
-                transpose_pass(flipped[:, h], w_halves[n][half][:, h, :], g)
+                if half == 0 and (n, g) in sorted_words:
+                    for u in range(2):
+                        nc.tensor.transpose(flipped[:, h, u, :], sorted_words[n, g][:, h, u, :], ident[:])
+                else:
+                    transpose_pass(flipped[:, h], w_halves[n][half][:, h, :], g)
             words = as_words(grouped_tiles[n, g][:])[:, half * HALF_COLS : (half + 1) * HALF_COLS, :]
             nc.scalar.copy(
                 out=words.rearrange("p (h c) u -> p h c u", h=HALF_HEADS),
@@ -180,25 +203,27 @@ def tile_jointattention_pa_kernel(tc, img, rope, w_qkv, out_q, out_k, out_v):
 
         def empty_bank(n, a, acc):
             by_head = acc.rearrange("p (h d) -> p h d", h=GROUP_HEADS)
-            nc.scalar.copy(out=result_tile(n)[:, ROTATED:, a, :], in_=by_head[:, ROTATED:, :])
-            result = result_tile(n)[:, 0:ROTATED, a, :]
-            cross = rot_pool.tile([P, ROTATED, PAIRS, 2], F32, name="cross")
+            count = ROTATED[n]
+            if count < GROUP_HEADS:
+                nc.scalar.copy(out=result_tile(n)[:, count:, a, :], in_=by_head[:, count:, :])
+            result = result_tile(n)[:, 0:count, a, :]
+            cross = rot_pool.tile([P, count, PAIRS, 2], F32, name="cross")
             crosses[n, a] = cross
             nc.vector.tensor_tensor(
                 out=cross[:],
-                in0=by_head[:, 0:ROTATED, :].rearrange("p h (i e) -> p h i e", e=2)[:, :, :, ::-1],
-                in1=sin_signed[:, a].unsqueeze(1).to_broadcast([P, ROTATED, PAIRS, 2]),
+                in0=by_head[:, 0:count, :].rearrange("p h (i e) -> p h i e", e=2)[:, :, :, ::-1],
+                in1=sin_signed[:, a].unsqueeze(1).to_broadcast([P, count, PAIRS, 2]),
                 op=MULT,
             )
             nc.vector.tensor_tensor(
                 out=result,
-                in0=by_head[:, 0:ROTATED, :],
-                in1=cos_twice[:, a, :].unsqueeze(1).to_broadcast([P, ROTATED, D]),
+                in0=by_head[:, 0:count, :],
+                in1=cos_twice[:, a, :].unsqueeze(1).to_broadcast([P, count, D]),
                 op=MULT,
             )
 
         def add_products(n, a):
-            result = result_tile(n)[:, 0:ROTATED, a, :]
+            result = result_tile(n)[:, 0 : ROTATED[n], a, :]
             cross = crosses.pop((n, a))
             engine = nc.gpsimd if a < GPSIMD_SUMS else nc.vector
             engine.tensor_tensor(
@@ -214,8 +239,10 @@ def tile_jointattention_pa_kernel(tc, img, rope, w_qkv, out_q, out_k, out_v):
             )
 
         def store_group(n):
-            store(n, ROTATED, GROUP_HEADS - ROTATED)
-            store(n, 0, ROTATED)
+            count = ROTATED[n]
+            if count < GROUP_HEADS:
+                store(n, count, GROUP_HEADS - count)
+            store(n, 0, count)
 
         products = [(n, a) for n in range(last) for a in range(TOKEN_TILES)]
         unsummed = []
@@ -250,6 +277,9 @@ def tile_jointattention_pa_kernel(tc, img, rope, w_qkv, out_q, out_k, out_v):
             for g in range(PASSES):
                 for half in range(2):
                     flip(n, g, half)
+                ahead = PASSES * n + g + SORT_AHEAD
+                if ahead % PASSES > 0 and ahead < PASSES * len(groups):
+                    sort_words(ahead // PASSES, ahead % PASSES)
                 quantise(n, g)
                 if (n, g) != (2, 0):
                     take_product()

from contextlib import ExitStack

from concourse import mybir
from concourse.masks import make_identity

F32 = mybir.dt.float32
BF16 = mybir.dt.bfloat16
U32 = mybir.dt.uint32
U8 = mybir.dt.uint8
FP8X4 = mybir.dt.float8_e4m3fn_x4
MULT = mybir.AluOpType.mult
ADD = mybir.AluOpType.add

P = 128
TOKENS = 384
HID = 1536
HEADS = 12
D = 128
K_PASS = 512
PASSES = HID // K_PASS
TOKEN_TILES = TOKENS // P
GROUP_HEADS = 4
GROUP_COLS = GROUP_HEADS * D
HALF_HEADS = GROUP_HEADS // 2
HALF_COLS = HALF_HEADS * D
PAIRS = D // 2
V_PART = 2
ROTATED = (4, 4, 4, 3, 3, 2, 2, 2, 0)
GPSIMD_SUMS = 2
SORT_AHEAD = 3

FLOPS = 2 * TOKENS * 3 * HEADS * D * HID


def tile_jointattention_pa_kernel(tc, img, rope, w_qkv, out_q, out_k, out_v):
    nc = tc.nc
    outs = [o.rearrange("b h n d -> (b h) n d") for o in (out_q, out_k, out_v)]
    rotated = [(part, head) for part in range(V_PART) for head in range(HEADS)]
    others = [(V_PART, head) for head in range(HEADS)]
    groups = []
    for n, count in enumerate(ROTATED):
        first = sum(ROTATED[:n])
        first_v = GROUP_HEADS * n - first
        groups.append(rotated[first : first + count] + others[first_v : first_v + GROUP_HEADS - count])
    last = len(groups) - 1

    with ExitStack() as stack:
        const = stack.enter_context(tc.tile_pool(name="const", bufs=1))
        w_pool = stack.enter_context(tc.tile_pool(name="w_rows", bufs=len(groups)))
        grouped_pool = stack.enter_context(tc.tile_pool(name="grouped", bufs=7))
        img_grouped_pool = stack.enter_context(tc.tile_pool(name="img_grouped", bufs=2))
        quant_pool = stack.enter_context(tc.tile_pool(name="quant", bufs=3))
        sorted_pool = stack.enter_context(tc.tile_pool(name="sorted", bufs=4))
        rot_pool = stack.enter_context(tc.tile_pool(name="rot", bufs=4))
        out_pool = stack.enter_context(tc.tile_pool(name="out", bufs=6))
        flip_psum = stack.enter_context(tc.psum_pool(name="flip", bufs=4))
        acc_psum = stack.enter_context(tc.psum_pool(name="acc", bufs=4))
        stack.enter_context(tc.manual_schedule())

        ident = const.tile([P, P], F32)
        make_identity(nc, ident[:])

        img_rows = img.flatten_outer_dims().rearrange("(p a) k -> p a k", a=TOKEN_TILES)
        img_sb = []
        for a in range(TOKEN_TILES):
            rows_sb = const.tile([P, HID], BF16, name=f"img_sb{a}")
            nc.sync.dma_start(out=rows_sb[:], in_=img_rows[:, a, :])
            img_sb.append(rows_sb)
        rope_sb = const.tile([P, TOKEN_TILES, D], BF16)
        w_halves = []
        for n, heads in enumerate(groups):
            halves = []
            for half in range(2):
                w_sb = w_pool.tile([P, HALF_HEADS, HID], BF16, name=f"w_sb{half}")
                pair = heads[half * HALF_HEADS : (half + 1) * HALF_HEADS]
                neighbours = pair[0][0] == pair[1][0]
                for h, count in [(0, 2)] if neighbours else [(0, 1), (1, 1)]:
                    part, head = pair[h]
                    first_row = (part * HEADS + head) * D
                    nc.sync.dma_start(
                        out=w_sb[:, h : h + count, :],
                        in_=w_qkv[first_row : first_row + count * D, :].rearrange("(h p) k -> p h k", p=P),
                    )
                halves.append(w_sb)
            w_halves.append(halves)
            if n == 0:
                nc.sync.dma_start(
                    out=rope_sb[:], in_=rope.flatten_outer_dims().rearrange("(p a) d -> p a d", a=TOKEN_TILES)
                )

        def transpose_pass(flipped, rows, g):
            first_word = (K_PASS // 2) * g
            for u in range(2):
                nc.tensor.transpose(
                    flipped[:, u, :], rows.bitcast(F32)[:, first_word + u : first_word + 2 * P : 2], ident[:]
                )

        def as_words(grouped):
            return grouped.rearrange("p c v -> p (c v)").bitcast(F32).rearrange("p (c u) -> p c u", u=2)

        img_codes = const.tile([P, TOKEN_TILES, PASSES, P], U32, align_bytes=64)
        img_scales = const.tile([P, TOKEN_TILES, PASSES, P], U8, align_bytes=64)
        for a in range(TOKEN_TILES):
            for first_g, count in ((0, 2), (2, 1)):
                flipped = flip_psum.tile([P, 2, 2, P], F32, name="flipped")
                for j in range(count):
                    transpose_pass(flipped[:, j], img_sb[a][:], first_g + j)
                img_grouped = img_grouped_pool.tile([P, count, P, 4], BF16, align_bytes=64, name=f"img_grouped{count}")
                nc.scalar.copy(
                    out=as_words(img_grouped[:].rearrange("p j c v -> p (j c) v")).rearrange(
                        "p (j c) u -> p j c u", j=count
                    ),
                    in_=flipped[:, 0:count].rearrange("p j u c -> p j c u"),
                )
                nc.vector.quantize_mx(
                    out=img_codes[:, a, first_g : first_g + count, :].rearrange("p g c -> p (g c)").bitcast(FP8X4),
                    scales=img_scales[:, a, first_g : first_g + count, :].rearrange("p g c -> p (g c)"),
                    in_=img_grouped[:].rearrange("p j c v -> p (j c v)"),
                )

        rope_pairs = rope_sb[:].rearrange("p a (i e) -> p a i e", e=2)
        cos_twice = const.tile([P, TOKEN_TILES, D], F32)
        sin_signed = const.tile([P, TOKEN_TILES, PAIRS, 2], F32)

        def make_tables():
            nc.vector.tensor_copy(
                out=cos_twice[:].rearrange("p a (i e) -> p a i e", e=2),
                in_=rope_pairs[:, :, :, 0:1].to_broadcast([P, TOKEN_TILES, PAIRS, 2]),
            )
            nc.vector.tensor_scalar_mul(out=sin_signed[:, :, :, 0], in0=rope_pairs[:, :, :, 1], scalar1=-1.0)
            nc.vector.tensor_copy(out=sin_signed[:, :, :, 1], in_=rope_pairs[:, :, :, 1])

        grouped_tiles = {}
        codes = {}
        results = {}
        crosses = {}

        sorted_words = {}

        def sort_words(n, g):
            tile = sorted_pool.tile([P, HALF_HEADS, 2, P], F32, name="sorted")
            sorted_words[n, g] = tile
            first_word = (K_PASS // 2) * g
            nc.scalar.copy(
                out=tile[:],
                in_=w_halves[n][0][:].bitcast(F32)[:, :, first_word : first_word + 2 * P].rearrange(
                    "p h (q u) -> p h u q", u=2
                ),
            )

        def flip(n, g, half):
            if (n, g) not in grouped_tiles:
                grouped_tiles[n, g] = grouped_pool.tile(
                    [P, GROUP_COLS, 4], BF16, align_bytes=64, name="w_grouped"
                )
            flipped = flip_psum.tile([P, 2, 2, P], F32, name="flipped")
            for h in range(HALF_HEADS):
                if half == 0 and (n, g) in sorted_words:
                    for u in range(2):
                        nc.tensor.transpose(flipped[:, h, u, :], sorted_words[n, g][:, h, u, :], ident[:])
                else:
                    transpose_pass(flipped[:, h], w_halves[n][half][:, h, :], g)
            words = as_words(grouped_tiles[n, g][:])[:, half * HALF_COLS : (half + 1) * HALF_COLS, :]
            nc.scalar.copy(
                out=words.rearrange("p (h c) u -> p h c u", h=HALF_HEADS),
                in_=flipped[:].rearrange("p h u c -> p h c u"),
            )

        def quantise(n, g):
            if n not in codes:
                codes[n] = (
                    quant_pool.tile([P, PASSES, GROUP_COLS], U32, align_bytes=64, name="w_codes"),
                    quant_pool.tile([P, PASSES, GROUP_COLS], U8, align_bytes=64, name="w_scales"),
                )
            nc.vector.quantize_mx(
                out=codes[n][0][:, g, :].bitcast(FP8X4),
                scales=codes[n][1][:, g, :],
                in_=grouped_tiles.pop((n, g))[:].rearrange("p c v -> p (c v)"),
            )

        def multiply(n, a, first_col, width):
            if n == last and (first_col == 0 or a == 0):
                acc = flip_psum.tile([P, 2, 2, P], F32, name="flipped")[:].rearrange("p h u c -> p (h u c)")
            else:
                acc = acc_psum.tile([P, GROUP_COLS], F32, name="acc")[:]
            cols = slice(first_col, first_col + width)
            for g in range(PASSES):
                nc.tensor.matmul_mx(
                    out=acc[:, 0:width],
                    lhsT=img_codes[:, a, g, :].bitcast(FP8X4),
                    lhsT_scale=img_scales[:, a, g, :],
                    rhs=codes[n][0][:, g, cols].bitcast(FP8X4),
                    rhs_scale=codes[n][1][:, g, cols],
                    start=(g == 0),
                    stop=(g == PASSES - 1),
                )
            return acc

        def result_tile(n):
            if n not in results:
                results[n] = out_pool.tile([P, GROUP_HEADS, TOKEN_TILES, D], F32, name="out_sb")
            return results[n]

        def empty_bank(n, a, acc):
            by_head = acc.rearrange("p (h d) -> p h d", h=GROUP_HEADS)
            count = ROTATED[n]
            if count < GROUP_HEADS:
                nc.scalar.copy(out=result_tile(n)[:, count:, a, :], in_=by_head[:, count:, :])
            result = result_tile(n)[:, 0:count, a, :]
            cross = rot_pool.tile([P, count, PAIRS, 2], F32, name="cross")
            crosses[n, a] = cross
            nc.vector.tensor_tensor(
                out=cross[:],
                in0=by_head[:, 0:count, :].rearrange("p h (i e) -> p h i e", e=2)[:, :, :, ::-1],
                in1=sin_signed[:, a].unsqueeze(1).to_broadcast([P, count, PAIRS, 2]),
                op=MULT,
            )
            nc.vector.tensor_tensor(
                out=result,
                in0=by_head[:, 0:count, :],
                in1=cos_twice[:, a, :].unsqueeze(1).to_broadcast([P, count, D]),
                op=MULT,
            )

        def add_products(n, a):
            result = result_tile(n)[:, 0 : ROTATED[n], a, :]
            cross = crosses.pop((n, a))
            engine = nc.gpsimd if a < GPSIMD_SUMS else nc.vector
            engine.tensor_tensor(
                out=result, in0=result, in1=cross[:].rearrange("p h i e -> p h (i e)"), op=ADD
            )

        def store(n, first_head, heads):
            which, head = groups[n][first_head]
            engine = nc.scalar if n == last else nc.sync
            engine.dma_start(
                out=outs[which][head : head + heads].rearrange("h (p a) d -> p h (a d)", a=TOKEN_TILES),
                in_=result_tile(n)[:, first_head : first_head + heads].rearrange("p h a d -> p h (a d)"),
            )

        def store_group(n):
            count = ROTATED[n]
            if count < GROUP_HEADS:
                store(n, count, GROUP_HEADS - count)
            store(n, 0, count)

        products = [(n, a) for n in range(last) for a in range(TOKEN_TILES)]
        unsummed = []

        def sum_products():
            for n, a in unsummed:
                add_products(n, a)
                if a == TOKEN_TILES - 1:
                    store_group(n)
            unsummed.clear()

        def take_product():
            n, a = products[0]
            products.remove(products[0])
            acc = multiply(n, a, 0, GROUP_COLS)
            sum_products()
            unsummed.append((n, a))
            empty_bank(n, a, acc)

        for n in range(2):
            for half in range(2):
                for g in range(PASSES):
                    flip(n, g, half)
                    if n == 0 and half == 0 and g == 0:
                        make_tables()
                    if half == 1:
                        quantise(n, g)
                if n == 1:
                    for i in range(2 * half):
                        take_product()
        for n in range(2, last + 1):
            for g in range(PASSES):
                for half in range(2):
                    flip(n, g, half)
                ahead = PASSES * n + g + SORT_AHEAD
                if ahead % PASSES > 0 and ahead < PASSES * len(groups):
                    sort_words(ahead // PASSES, ahead % PASSES)
                quantise(n, g)
                if (n, g) != (2, 0):
                    take_product()
        while products:
            take_product()
        sum_products()
        for half in range(2):
            for a in range(TOKEN_TILES):
                acc = multiply(last, a, half * HALF_COLS, HALF_COLS)
                heads = slice(half * HALF_HEADS, (half + 1) * HALF_HEADS)
                nc.scalar.copy(
                    out=result_tile(last)[:, heads, a, :],
                    in_=acc[:, 0:HALF_COLS].rearrange("p (h d) -> p h d", h=HALF_HEADS),
                )
            store(last, half * HALF_HEADS, HALF_HEADS)
